import numpy as np
import ml_dtypes


def mxq(x, axis, fmt="e4m3"):
    dtype, down = {"e4m3": (ml_dtypes.float8_e4m3fn, 7), "e5m2": (ml_dtypes.float8_e5m2, 14)}[fmt]
    v = np.moveaxis(np.asarray(x, np.float32).astype(ml_dtypes.bfloat16).astype(np.float64), axis, -1)
    blocks = v.reshape(v.shape[:-1] + (-1, 32))
    amax = np.abs(blocks).max(-1, keepdims=True)
    byte = np.maximum(np.where(amax > 0, np.frexp(amax)[1] - 1 + 127, 0) - down, 1)
    scale = np.exp2(byte - 127.0)
    codes = (blocks / scale).astype(np.float32).astype(dtype).astype(np.float64)
    return np.moveaxis((codes * scale).reshape(v.shape), -1, axis)


WIDE = False


def mx_kscale(k):
    if not WIDE:
        return np.ones(k)
    levels = np.array([10, -10, 5, -5, 0])
    if k % 512:
        return np.exp2(np.random.permutation(np.resize(levels, k // 32))).repeat(32)
    a = np.empty((k // 512, 16))
    for p in range(k // 512):
        a[p, :8] = np.random.permutation(np.resize(levels, 8))
        for g in range(8):
            far = levels[np.abs(levels - a[p, g]) >= 10]
            a[p, g + 8] = far[np.random.randint(len(far))]
    return np.exp2(a.ravel()).repeat(32)


BF16 = ml_dtypes.bfloat16


def bf(x):
    return np.asarray(x, np.float32).astype(BF16)


def f64(x):
    return np.asarray(x).astype(np.float64)


B, L, E, QH, KVH, D, FFN = 2, 2048, 512, 8, 1, 128, 1024
KV = KVH * D
EPS = 1.1920928955078125e-07


def rmsnorm(x, w):
    return x / np.sqrt(np.mean(x * x, axis=-1, keepdims=True) + EPS) * w


def setup_inputs():
    s, t = mx_kscale(FFN), mx_kscale(E)
    return {"ffn_act": bf(np.random.standard_normal((B, L, FFN)) * 0.6 * s),
            "wd": bf(np.random.standard_normal((FFN, E)) / np.sqrt(FFN) / s[:, None]),
            "residual": bf(np.random.standard_normal((B, L, E)) * 1.1),
            "ln1_w": bf((1.0 + 0.1 * np.random.standard_normal(E)) * t),
            "wk": bf(np.random.standard_normal((E, KV)) / np.sqrt(E) / t[:, None]),
            "wv": bf(np.random.standard_normal((E, KV)) / np.sqrt(E) / t[:, None])}


def reference(ffn_act, wd, residual, ln1_w, wk, wv):
    x_out = (mxq(f64(ffn_act), 2, "e4m3") @ mxq(f64(wd), 0, "e4m3")) + f64(residual)
    hq = mxq(rmsnorm(x_out, f64(ln1_w)), 2, "e4m3")
    k_out = (hq @ mxq(f64(wk), 0, "e4m3")).reshape(B, L, KV)
    v_out = (hq @ mxq(f64(wv), 0, "e4m3")).reshape(B, L, KV)
    return x_out, k_out, v_out

@@ -1,0 +1,291 @@
+from contextlib import ExitStack
+
+import concourse.mybir as mybir
+from concourse.masks import make_identity
+
+F32 = mybir.dt.float32
+BF16 = mybir.dt.bfloat16
+U32 = mybir.dt.uint32
+U8 = mybir.dt.uint8
+FP8X4 = mybir.dt.float8_e4m3fn_x4
+ACT = mybir.ActivationFunctionType
+ALU = mybir.AluOpType
+
+P = 128
+PACK = 4
+K_PASS = P * PACK
+
+TOKENS = 4096
+FFN = 1024
+E = 512
+KV = 128
+EPS = 2.0**-23
+DOWN_PASSES = FFN // K_PASS
+
+TILES = TOKENS // P
+PAIR = 2
+CHUNK_TILES = 4
+CHUNK = CHUNK_TILES * P
+
+FLOPS = 2 * TOKENS * FFN * E + 2 * TOKENS * E * (2 * KV)
+
+
+def tile_textencoderblock_pc_t_kernel(
+    tc, ffn_act, wd, residual, ln1_w, wk, wv, out_0, out_1, out_2
+):
+    nc = tc.nc
+    a_rows = ffn_act.flatten_outer_dims()
+    res_rows = residual.flatten_outer_dims()
+    x_rows = out_0.flatten_outer_dims()
+    k_rows = out_1.flatten_outer_dims()
+    v_rows = out_2.flatten_outer_dims()
+
+    def chunk_view(rows, c):
+        return rows[c * CHUNK : (c + 1) * CHUNK, :].rearrange("(p j) w -> p j w", j=CHUNK_TILES)
+
+    def pair_view(rows, s):
+        j0 = s % CHUNK_TILES
+        return chunk_view(rows, s // CHUNK_TILES)[:, j0 : j0 + PAIR, :]
+
+    with ExitStack() as ctx:
+        consts = ctx.enter_context(tc.tile_pool(name="consts", bufs=1))
+        a_pool = ctx.enter_context(tc.tile_pool(name="a", bufs=TILES))
+        res_pool = ctx.enter_context(tc.tile_pool(name="res", bufs=TILES // CHUNK_TILES))
+        grouped_pool = ctx.enter_context(tc.tile_pool(name="grouped", bufs=3))
+        mx_pool = ctx.enter_context(tc.tile_pool(name="mx", bufs=2))
+        x_pool = ctx.enter_context(tc.tile_pool(name="x", bufs=10))
+        stat_pool = ctx.enter_context(tc.tile_pool(name="stat", bufs=4))
+        square_pool = ctx.enter_context(tc.tile_pool(name="square", bufs=4))
+        h_pool = ctx.enter_context(tc.tile_pool(name="h", bufs=3))
+        kv_pool = ctx.enter_context(tc.tile_pool(name="kv", bufs=10))
+        psum_gain = ctx.enter_context(tc.psum_pool(name="psum_gain", bufs=1))
+        psum_a = ctx.enter_context(tc.psum_pool(name="psum_a", bufs=2))
+        psum_x = ctx.enter_context(tc.psum_pool(name="psum_x", bufs=2))
+        psum_h = ctx.enter_context(tc.psum_pool(name="psum_h", bufs=1))
+        psum_kv = ctx.enter_context(tc.psum_pool(name="psum_kv", bufs=2))
+        ctx.enter_context(tc.manual_schedule())
+
+        a_of, res_of, aT_of, a_grouped_of, a_mx_of, x_psum_of, x_of = {}, {}, {}, {}, {}, {}, {}
+        rstd_of, h_of, hT_of, h_grouped_of, h_mx_of, kv_psum_of, kv_of = {}, {}, {}, {}, {}, {}, {}
+
+        ident = consts.tile([P, P], F32)
+        make_identity(nc, ident[:])
+        ones = consts.tile([P, P], BF16)
+        nc.vector.memset(ones[:], 1.0)
+        gain_row = consts.tile([P, E], BF16)
+        nc.vector.memset(gain_row[:], 0.0)
+        minus_half = consts.tile([P, 1], F32)
+        nc.vector.memset(minus_half[:], -0.5)
+        table_warmer = consts.tile([P, 1], F32)
+        nc.scalar.activation(out=table_warmer[:], in_=minus_half[:], func=ACT.Square)
+
+        def load_weight_pass(rows, raw):
+            nc.sync.dma_start(out=raw, in_=rows.rearrange("(p t) n -> p t n", t=PACK))
+
+        def load_chunk(c):
+            for j in range(CHUNK_TILES):
+                a_sb = a_pool.tile([P, FFN], BF16)
+                nc.sync.dma_start(out=a_sb[:], in_=chunk_view(a_rows, c)[:, j, :])
+                a_of[c * CHUNK_TILES + j] = a_sb
+            res_sb = res_pool.tile([P, CHUNK_TILES, E], BF16)
+            nc.sync.dma_start(out=res_sb[:], in_=chunk_view(res_rows, c))
+            res_of[c] = res_sb
+
+        wd_raw = consts.tile([P, DOWN_PASSES, PACK, E], BF16)
+        wkv_raw = consts.tile([P, 2, PACK, KV], BF16)
+        for g in range(DOWN_PASSES):
+            load_weight_pass(wd[g * K_PASS : (g + 1) * K_PASS, :], wd_raw[:, g])
+        load_chunk(0)
+        nc.sync.dma_start(out=gain_row[0:1, :], in_=ln1_w.unsqueeze(0))
+        load_weight_pass(wk, wkv_raw[:, 0])
+        load_weight_pass(wv, wkv_raw[:, 1])
+        for c in range(1, TILES // CHUNK_TILES):
+            load_chunk(c)
+
+        def group_weight(raw, grouped):
+            nc.vector.tensor_copy(
+                out=grouped.rearrange("p (c i) t -> p c t i", i=4),
+                in_=raw.rearrange("p t (c i) -> p c t i", i=4),
+            )
+
+        wd_grouped = consts.tile([P, DOWN_PASSES, E, PACK], BF16, align_bytes=64)
+        wd_codes = consts.tile([P, DOWN_PASSES, E], U32, align_bytes=64)
+        wd_scales = consts.tile([P, DOWN_PASSES, E], U8, align_bytes=64)
+        for g in range(DOWN_PASSES):
+            group_weight(wd_raw[:, g], wd_grouped[:, g])
+        for g in range(DOWN_PASSES):
+            nc.vector.quantize_mx(
+                out=wd_codes[:, g, :].bitcast(FP8X4),
+                scales=wd_scales[:, g, :],
+                in_=wd_grouped[:, g].rearrange("p n t -> p (n t)"),
+            )
+
+        wkv_grouped = consts.tile([P, 2, KV, PACK], BF16, align_bytes=64)
+        wkv_codes = consts.tile([P, 2 * KV], U32, align_bytes=64)
+        wkv_scales = consts.tile([P, 2 * KV], U8, align_bytes=64)
+
+        gain = psum_gain.tile([P, E], F32)
+
+        def prepare_norm_and_kv():
+            nc.tensor.matmul(out=gain[:], lhsT=ones[:], rhs=gain_row[:], start=True, stop=True)
+            for s in range(2):
+                group_weight(wkv_raw[:, s], wkv_grouped[:, s])
+            nc.vector.quantize_mx(
+                out=wkv_codes[:].bitcast(FP8X4),
+                scales=wkv_scales[:],
+                in_=wkv_grouped[:].rearrange("p s n t -> p (s n t)"),
+            )
+
+        def transpose_a(s):
+            a_words = a_of[s][:].bitcast(F32)
+            aT = psum_a.tile([P, PACK * P], F32)
+            for gu in range(PACK):
+                g, u = divmod(gu, 2)
+                words = slice(2 * P * g + u, 2 * P * (g + 1), 2)
+                nc.tensor.transpose(aT[:, gu * P : (gu + 1) * P], a_words[:, words], ident[:])
+            aT_of[s] = aT
+
+        def group_a(s):
+            a_grouped = grouped_pool.tile([P, FFN], BF16, align_bytes=64)
+            nc.scalar.copy(
+                out=a_grouped[:].bitcast(F32).rearrange("p (g r u) -> p g r u", g=DOWN_PASSES, u=2),
+                in_=aT_of[s][:].rearrange("p (g u r) -> p g r u", g=DOWN_PASSES, u=2),
+            )
+            a_grouped_of[s] = a_grouped
+
+        def quantise_a(s):
+            a_codes = mx_pool.tile([P, DOWN_PASSES * P], U32, align_bytes=64)
+            a_scales = mx_pool.tile([P, DOWN_PASSES * P], U8, align_bytes=64)
+            nc.vector.quantize_mx(
+                out=a_codes[:].bitcast(FP8X4), scales=a_scales[:], in_=a_grouped_of[s][:]
+            )
+            a_mx_of[s] = (a_codes, a_scales)
+
+        def project_down(s):
+            a_codes, a_scales = a_mx_of[s]
+            x_psum = psum_x.tile([P, E], F32)
+            for g in range(DOWN_PASSES):
+                cols = slice(g * P, (g + 1) * P)
+                nc.tensor.matmul_mx(
+                    out=x_psum[:],
+                    lhsT=a_codes[:, cols].bitcast(FP8X4),
+                    lhsT_scale=a_scales[:, cols],
+                    rhs=wd_codes[:, g, :].bitcast(FP8X4),
+                    rhs_scale=wd_scales[:, g, :],
+                    start=(g == 0),
+                    stop=(g == DOWN_PASSES - 1),
+                )
+            x_psum_of[s] = x_psum
+
+        def add_residual(s):
+            if s % PAIR == 0:
+                x_sb = x_pool.tile([P, PAIR, E], F32)
+                x_of[s // PAIR] = x_sb
+            nc.vector.tensor_tensor(
+                out=x_of[s // PAIR][:, s % PAIR, :],
+                in0=x_psum_of[s][:],
+                in1=res_of[s // CHUNK_TILES][:, s % CHUNK_TILES, :],
+                op=ALU.add,
+            )
+            if s % PAIR == PAIR - 1:
+                nc.sync.dma_start(out=pair_view(x_rows, s - (PAIR - 1)), in_=x_of[s // PAIR][:])
+
+        def inverse_rms(s):
+            squares = square_pool.tile([P, E], BF16)
+            sum_sq = stat_pool.tile([P, 1], F32)
+            nc.scalar.activation(
+                out=squares[:], in_=x_of[s // PAIR][:, s % PAIR, :], func=ACT.Square, accum_out=sum_sq[:]
+            )
+            mean_sq = stat_pool.tile([P, 1], F32)
+            nc.gpsimd.tensor_scalar(
+                out=mean_sq[:], in0=sum_sq[:], scalar1=1.0 / E, scalar2=EPS, op0=ALU.mult, op1=ALU.add
+            )
+            rstd = stat_pool.tile([P, 1], F32)
+            nc.gpsimd.tensor_tensor(out=rstd[:], in0=mean_sq[:], in1=minus_half[:], op=ALU.pow)
+            rstd_of[s] = rstd
+
+        def normalise(s):
+            h_sb = h_pool.tile([P, E], BF16)
+            nc.vector.scalar_tensor_tensor(
+                out=h_sb[:],
+                in0=x_of[s // PAIR][:, s % PAIR, :],
+                scalar=rstd_of[s][:],
+                in1=gain[:],
+                op0=ALU.mult,
+                op1=ALU.mult,
+            )
+            h_of[s] = h_sb
+
+        def transpose_h(s):
+            h_words = h_of[s][:].bitcast(F32)
+            hT = psum_h.tile([P, 2 * P], F32)
+            for u in range(2):
+                words = slice(u, 2 * P, 2)
+                nc.tensor.transpose(hT[:, u * P : (u + 1) * P], h_words[:, words], ident[:])
+            hT_of[s] = hT
+
+        def group_h(s):
+            h_grouped = grouped_pool.tile([P, E], BF16, align_bytes=64)
+            nc.scalar.copy(
+                out=h_grouped[:].bitcast(F32).rearrange("p (r u) -> p r u", u=2),
+                in_=hT_of[s][:].rearrange("p (u r) -> p r u", u=2),
+            )
+            h_grouped_of[s] = h_grouped
+
+        def quantise_h(s):
+            h_codes = mx_pool.tile([P, P], U32, align_bytes=64)
+            h_scales = mx_pool.tile([P, P], U8, align_bytes=64)
+            nc.vector.quantize_mx(
+                out=h_codes[:].bitcast(FP8X4), scales=h_scales[:], in_=h_grouped_of[s][:]
+            )
+            h_mx_of[s] = (h_codes, h_scales)
+
+        def project_kv(s):
+            h_codes, h_scales = h_mx_of[s]
+            kv_psum = psum_kv.tile([P, 2 * KV], F32)
+            nc.tensor.matmul_mx(
+                out=kv_psum[:],
+                lhsT=h_codes[:].bitcast(FP8X4),
+                lhsT_scale=h_scales[:],
+                rhs=wkv_codes[:].bitcast(FP8X4),
+                rhs_scale=wkv_scales[:],
+                start=True,
+                stop=True,
+            )
+            kv_psum_of[s] = kv_psum
+
+        def store_kv(s):
+            if s % PAIR == 0:
+                kv_sb = kv_pool.tile([P, 2, PAIR, KV], F32)
+                kv_of[s // PAIR] = kv_sb
+            nc.scalar.copy(
+                out=kv_of[s // PAIR][:, :, s % PAIR, :],
+                in_=kv_psum_of[s][:].rearrange("p (o d) -> p o d", o=2),
+            )
+            if s % PAIR == PAIR - 1:
+                nc.sync.dma_start(out=pair_view(k_rows, s - (PAIR - 1)), in_=kv_of[s // PAIR][:, 0])
+                nc.sync.dma_start(out=pair_view(v_rows, s - (PAIR - 1)), in_=kv_of[s // PAIR][:, 1])
+
+        def run(stage, s):
+            if 0 <= s < TILES:
+                stage(s)
+
+        def step(t):
+            run(transpose_h, t - 3)
+            run(transpose_a, t + 5)
+            run(add_residual, t)
+            run(inverse_rms, t)
+            run(quantise_h, t - 5)
+            run(normalise, t - 2)
+            run(group_a, t + 4)
+            run(group_h, t - 3)
+            run(store_kv, t - 6)
+            run(project_kv, t - 5)
+            run(quantise_a, t + 2)
+            run(project_down, t + 2)
+
+        for t in range(-5, 1):
+            step(t)
+        prepare_norm_and_kv()
+        for t in range(1, TILES + 6):
+            step(t)

@@ -129,7 +129,10 @@ def tile_textencoderblock_pc_t_kernel(
         def prepare_norm_and_kv():
             nc.tensor.matmul(out=gain[:], lhsT=ones[:], rhs=gain_row[:], start=True, stop=True)
             for s in range(2):
-                group_weight(wkv_raw[:, s], wkv_grouped[:, s])
+                nc.vector.tensor_copy(
+                    out=wkv_grouped[:, s].rearrange("p n (u e) -> p n u e", u=2),
+                    in_=wkv_raw[:, s].rearrange("p (e u) n -> p n u e", u=2),
+                )
             nc.vector.quantize_mx(
                 out=wkv_codes[:].bitcast(FP8X4),
                 scales=wkv_scales[:],
@@ -207,10 +210,10 @@ def tile_textencoderblock_pc_t_kernel(
         def normalise(s):
             h_sb = h_pool.tile([P, E], BF16)
             nc.vector.scalar_tensor_tensor(
-                out=h_sb[:],
-                in0=x_of[s // PAIR][:, s % PAIR, :],
+                out=h_sb[:].rearrange("p (u j) -> p u j", u=2),
+                in0=x_of[s // PAIR][:, s % PAIR, :].rearrange("p (j u) -> p u j", u=2),
                 scalar=rstd_of[s][:],
-                in1=gain[:],
+                in1=gain[:].rearrange("p (j u) -> p u j", u=2),
                 op0=ALU.mult,
                 op1=ALU.mult,
             )
@@ -220,8 +223,8 @@ def tile_textencoderblock_pc_t_kernel(
             h_words = h_of[s][:].bitcast(F32)
             hT = psum_h.tile([P, 2 * P], F32)
             for u in range(2):
-                words = slice(u, 2 * P, 2)
-                nc.tensor.transpose(hT[:, u * P : (u + 1) * P], h_words[:, words], ident[:])
+                cols = slice(u * P, (u + 1) * P)
+                nc.tensor.transpose(hT[:, cols], h_words[:, cols], ident[:])
             hT_of[s] = hT
 
         def group_h(s):

@@ -23,9 +23,9 @@ EPS = 2.0**-23
 DOWN_PASSES = FFN // K_PASS
 
 TILES = TOKENS // P
-PAIR = 2
 CHUNK_TILES = 4
 CHUNK = CHUNK_TILES * P
+GROUPS = [[s, s + 1] for s in range(0, TILES, 2)]
 
 FLOPS = 2 * TOKENS * FFN * E + 2 * TOKENS * E * (2 * KV)
 
@@ -43,9 +43,9 @@ def tile_textencoderblock_pc_t_kernel(
     def chunk_view(rows, c):
         return rows[c * CHUNK : (c + 1) * CHUNK, :].rearrange("(p j) w -> p j w", j=CHUNK_TILES)
 
-    def pair_view(rows, s):
-        j0 = s % CHUNK_TILES
-        return chunk_view(rows, s // CHUNK_TILES)[:, j0 : j0 + PAIR, :]
+    def group_view(rows, tiles):
+        j0 = tiles[0] % CHUNK_TILES
+        return chunk_view(rows, tiles[0] // CHUNK_TILES)[:, j0 : j0 + len(tiles), :]
 
     with ExitStack() as ctx:
         consts = ctx.enter_context(tc.tile_pool(name="consts", bufs=1))
@@ -62,11 +62,11 @@ def tile_textencoderblock_pc_t_kernel(
         psum_a = ctx.enter_context(tc.psum_pool(name="psum_a", bufs=2))
         psum_x = ctx.enter_context(tc.psum_pool(name="psum_x", bufs=2))
         psum_h = ctx.enter_context(tc.psum_pool(name="psum_h", bufs=1))
-        psum_kv = ctx.enter_context(tc.psum_pool(name="psum_kv", bufs=2))
+        psum_kv = ctx.enter_context(tc.psum_pool(name="psum_kv", bufs=1))
         ctx.enter_context(tc.manual_schedule())
 
         a_of, res_of, aT_of, a_grouped_of, a_mx_of, x_psum_of, x_of = {}, {}, {}, {}, {}, {}, {}
-        rstd_of, h_of, hT_of, h_grouped_of, h_mx_of, kv_psum_of, kv_of = {}, {}, {}, {}, {}, {}, {}
+        sum_of, rstd_of, h_of, hT_of, h_grouped_of, h_mx_of, kv_psum_of = {}, {}, {}, {}, {}, {}, {}
 
         ident = consts.tile([P, P], F32)
         make_identity(nc, ident[:])
@@ -74,10 +74,10 @@ def tile_textencoderblock_pc_t_kernel(
         nc.vector.memset(ones[:], 1.0)
         gain_row = consts.tile([P, E], BF16)
         nc.vector.memset(gain_row[:], 0.0)
-        minus_half = consts.tile([P, 1], F32)
+        minus_half = consts.tile([P, 2], F32)
         nc.vector.memset(minus_half[:], -0.5)
         table_warmer = consts.tile([P, 1], F32)
-        nc.scalar.activation(out=table_warmer[:], in_=minus_half[:], func=ACT.Square)
+        nc.scalar.activation(out=table_warmer[:], in_=minus_half[:, 0:1], func=ACT.Square)
 
         def load_weight_pass(rows, raw):
             nc.sync.dma_start(out=raw, in_=rows.rearrange("(p t) n -> p t n", t=PACK))
@@ -139,156 +139,188 @@ def tile_textencoderblock_pc_t_kernel(
                 in_=wkv_grouped[:].rearrange("p s n t -> p (s n t)"),
             )
 
-        def transpose_a(s):
-            a_words = a_of[s][:].bitcast(F32)
-            aT = psum_a.tile([P, PACK * P], F32)
-            for gu in range(PACK):
-                g, u = divmod(gu, 2)
-                words = slice(2 * P * g + u, 2 * P * (g + 1), 2)
-                nc.tensor.transpose(aT[:, gu * P : (gu + 1) * P], a_words[:, words], ident[:])
-            aT_of[s] = aT
+        def transpose_a(g):
+            for s in GROUPS[g]:
+                a_words = a_of[s][:].bitcast(F32)
+                aT = psum_a.tile([P, PACK * P], F32)
+                for ku in range(PACK):
+                    k, u = divmod(ku, 2)
+                    words = slice(2 * P * k + u, 2 * P * (k + 1), 2)
+                    nc.tensor.transpose(aT[:, ku * P : (ku + 1) * P], a_words[:, words], ident[:])
+                aT_of[s] = aT
 
-        def group_a(s):
-            a_grouped = grouped_pool.tile([P, FFN], BF16, align_bytes=64)
+        def group_a(g, i):
+            if i >= len(GROUPS[g]):
+                return
+            if i == 0:
+                a_grouped = grouped_pool.tile([P, 2, FFN], BF16, align_bytes=64)
+                a_grouped_of[g] = a_grouped
             nc.scalar.copy(
-                out=a_grouped[:].bitcast(F32).rearrange("p (g r u) -> p g r u", g=DOWN_PASSES, u=2),
-                in_=aT_of[s][:].rearrange("p (g u r) -> p g r u", g=DOWN_PASSES, u=2),
+                out=a_grouped_of[g][:, i, :].bitcast(F32).rearrange("p (g r u) -> p g r u", g=DOWN_PASSES, u=2),
+                in_=aT_of[GROUPS[g][i]][:].rearrange("p (g u r) -> p g r u", g=DOWN_PASSES, u=2),
             )
-            a_grouped_of[s] = a_grouped
 
-        def quantise_a(s):
-            a_codes = mx_pool.tile([P, DOWN_PASSES * P], U32, align_bytes=64)
-            a_scales = mx_pool.tile([P, DOWN_PASSES * P], U8, align_bytes=64)
+        def quantise_a(g):
+            n = len(GROUPS[g])
+            a_codes = mx_pool.tile([P, 2 * DOWN_PASSES * P], U32, align_bytes=64)
+            a_scales = mx_pool.tile([P, 2 * DOWN_PASSES * P], U8, align_bytes=64)
             nc.vector.quantize_mx(
-                out=a_codes[:].bitcast(FP8X4), scales=a_scales[:], in_=a_grouped_of[s][:]
+                out=a_codes[:, : n * DOWN_PASSES * P].bitcast(FP8X4),
+                scales=a_scales[:, : n * DOWN_PASSES * P],
+                in_=a_grouped_of[g][:].rearrange("p i k -> p (i k)")[:, : n * FFN],
             )
-            a_mx_of[s] = (a_codes, a_scales)
+            a_mx_of[g] = (a_codes, a_scales)
 
-        def project_down(s):
-            a_codes, a_scales = a_mx_of[s]
-            x_psum = psum_x.tile([P, E], F32)
-            for g in range(DOWN_PASSES):
-                cols = slice(g * P, (g + 1) * P)
-                nc.tensor.matmul_mx(
-                    out=x_psum[:],
-                    lhsT=a_codes[:, cols].bitcast(FP8X4),
-                    lhsT_scale=a_scales[:, cols],
-                    rhs=wd_codes[:, g, :].bitcast(FP8X4),
-                    rhs_scale=wd_scales[:, g, :],
-                    start=(g == 0),
-                    stop=(g == DOWN_PASSES - 1),
-                )
-            x_psum_of[s] = x_psum
+        def project_down(g):
+            a_codes, a_scales = a_mx_of[g]
+            for i, s in enumerate(GROUPS[g]):
+                x_psum = psum_x.tile([P, E], F32)
+                for k in range(DOWN_PASSES):
+                    cols = slice((i * DOWN_PASSES + k) * P, (i * DOWN_PASSES + k + 1) * P)
+                    nc.tensor.matmul_mx(
+                        out=x_psum[:],
+                        lhsT=a_codes[:, cols].bitcast(FP8X4),
+                        lhsT_scale=a_scales[:, cols],
+                        rhs=wd_codes[:, k, :].bitcast(FP8X4),
+                        rhs_scale=wd_scales[:, k, :],
+                        start=(k == 0),
+                        stop=(k == DOWN_PASSES - 1),
+                    )
+                x_psum_of[s] = x_psum
 
-        def add_residual(s):
-            if s % PAIR == 0:
-                x_sb = x_pool.tile([P, PAIR, E], F32)
-                x_of[s // PAIR] = x_sb
+        def add_residual(g, i):
+            n = len(GROUPS[g])
+            if i >= n:
+                return
+            s = GROUPS[g][i]
+            if i == 0:
+                x_sb = x_pool.tile([P, 2, E], F32)
+                x_of[g] = x_sb
             nc.vector.tensor_tensor(
-                out=x_of[s // PAIR][:, s % PAIR, :],
+                out=x_of[g][:, i, :],
                 in0=x_psum_of[s][:],
                 in1=res_of[s // CHUNK_TILES][:, s % CHUNK_TILES, :],
                 op=ALU.add,
             )
-            if s % PAIR == PAIR - 1:
-                nc.sync.dma_start(out=pair_view(x_rows, s - (PAIR - 1)), in_=x_of[s // PAIR][:])
+            if i == n - 1:
+                nc.sync.dma_start(out=group_view(x_rows, GROUPS[g]), in_=x_of[g][:, :n, :])
 
-        def inverse_rms(s):
+        def sum_squares(g, i):
+            if i >= len(GROUPS[g]):
+                return
+            if i == 0:
+                sum_sq = stat_pool.tile([P, 2], F32)
+                sum_of[g] = sum_sq
             squares = square_pool.tile([P, E], BF16)
-            sum_sq = stat_pool.tile([P, 1], F32)
             nc.scalar.activation(
-                out=squares[:], in_=x_of[s // PAIR][:, s % PAIR, :], func=ACT.Square, accum_out=sum_sq[:]
+                out=squares[:], in_=x_of[g][:, i, :], func=ACT.Square, accum_out=sum_of[g][:, i : i + 1]
             )
-            mean_sq = stat_pool.tile([P, 1], F32)
-            nc.gpsimd.tensor_scalar(
-                out=mean_sq[:], in0=sum_sq[:], scalar1=1.0 / E, scalar2=EPS, op0=ALU.mult, op1=ALU.add
-            )
-            rstd = stat_pool.tile([P, 1], F32)
-            nc.gpsimd.tensor_tensor(out=rstd[:], in0=mean_sq[:], in1=minus_half[:], op=ALU.pow)
-            rstd_of[s] = rstd
 
-        def normalise(s):
-            h_sb = h_pool.tile([P, E], BF16)
+        def inverse_rms(g):
+            n = len(GROUPS[g])
+            mean_sq = stat_pool.tile([P, 2], F32)
+            nc.gpsimd.tensor_scalar(
+                out=mean_sq[:, :n], in0=sum_of[g][:, :n], scalar1=1.0 / E, scalar2=EPS, op0=ALU.mult, op1=ALU.add
+            )
+            rstd = stat_pool.tile([P, 2], F32)
+            nc.gpsimd.tensor_tensor(out=rstd[:, :n], in0=mean_sq[:, :n], in1=minus_half[:, :n], op=ALU.pow)
+            rstd_of[g] = rstd
+
+        def normalise(g, i):
+            if i >= len(GROUPS[g]):
+                return
+            if i == 0:
+                h_sb = h_pool.tile([P, 2, E], BF16)
+                h_of[g] = h_sb
             nc.vector.scalar_tensor_tensor(
-                out=h_sb[:].rearrange("p (u j) -> p u j", u=2),
-                in0=x_of[s // PAIR][:, s % PAIR, :].rearrange("p (j u) -> p u j", u=2),
-                scalar=rstd_of[s][:],
+                out=h_of[g][:, i, :].rearrange("p (u j) -> p u j", u=2),
+                in0=x_of[g][:, i, :].rearrange("p (j u) -> p u j", u=2),
+                scalar=rstd_of[g][:, i : i + 1],
                 in1=gain[:].rearrange("p (j u) -> p u j", u=2),
                 op0=ALU.mult,
                 op1=ALU.mult,
             )
-            h_of[s] = h_sb
 
-        def transpose_h(s):
-            h_words = h_of[s][:].bitcast(F32)
-            hT = psum_h.tile([P, 2 * P], F32)
-            for u in range(2):
-                cols = slice(u * P, (u + 1) * P)
-                nc.tensor.transpose(hT[:, cols], h_words[:, cols], ident[:])
-            hT_of[s] = hT
+        def transpose_h(g):
+            hT = psum_h.tile([P, 2, 2 * P], F32)
+            for i in range(len(GROUPS[g])):
+                h_words = h_of[g][:, i, :].bitcast(F32)
+                for u in range(2):
+                    cols = slice(u * P, (u + 1) * P)
+                    nc.tensor.transpose(hT[:, i, cols], h_words[:, cols], ident[:])
+            hT_of[g] = hT
 
-        def group_h(s):
-            h_grouped = grouped_pool.tile([P, E], BF16, align_bytes=64)
+        def group_h(g):
+            n = len(GROUPS[g])
+            h_grouped = grouped_pool.tile([P, 2, E], BF16, align_bytes=64)
             nc.scalar.copy(
-                out=h_grouped[:].bitcast(F32).rearrange("p (r u) -> p r u", u=2),
-                in_=hT_of[s][:].rearrange("p (u r) -> p r u", u=2),
+                out=h_grouped[:, :n, :].bitcast(F32).rearrange("p i (r u) -> p i r u", u=2),
+                in_=hT_of[g][:, :n, :].rearrange("p i (u r) -> p i r u", u=2),
             )
-            h_grouped_of[s] = h_grouped
+            h_grouped_of[g] = h_grouped
 
-        def quantise_h(s):
-            h_codes = mx_pool.tile([P, P], U32, align_bytes=64)
-            h_scales = mx_pool.tile([P, P], U8, align_bytes=64)
+        def quantise_h(g):
+            n = len(GROUPS[g])
+            h_codes = mx_pool.tile([P, 2 * P], U32, align_bytes=64)
+            h_scales = mx_pool.tile([P, 2 * P], U8, align_bytes=64)
             nc.vector.quantize_mx(
-                out=h_codes[:].bitcast(FP8X4), scales=h_scales[:], in_=h_grouped_of[s][:]
+                out=h_codes[:, : n * P].bitcast(FP8X4),
+                scales=h_scales[:, : n * P],
+                in_=h_grouped_of[g][:].rearrange("p i k -> p (i k)")[:, : n * E],
             )
-            h_mx_of[s] = (h_codes, h_scales)
+            h_mx_of[g] = (h_codes, h_scales)
 
-        def project_kv(s):
-            h_codes, h_scales = h_mx_of[s]
-            kv_psum = psum_kv.tile([P, 2 * KV], F32)
-            nc.tensor.matmul_mx(
-                out=kv_psum[:],
-                lhsT=h_codes[:].bitcast(FP8X4),
-                lhsT_scale=h_scales[:],
-                rhs=wkv_codes[:].bitcast(FP8X4),
-                rhs_scale=wkv_scales[:],
-                start=True,
-                stop=True,
-            )
-            kv_psum_of[s] = kv_psum
+        def project_kv(g):
+            h_codes, h_scales = h_mx_of[g]
+            kv_psum = psum_kv.tile([P, 2, 2 * KV], F32)
+            for i in range(len(GROUPS[g])):
+                cols = slice(i * P, (i + 1) * P)
+                nc.tensor.matmul_mx(
+                    out=kv_psum[:, i, :],
+                    lhsT=h_codes[:, cols].bitcast(FP8X4),
+                    lhsT_scale=h_scales[:, cols],
+                    rhs=wkv_codes[:].bitcast(FP8X4),
+                    rhs_scale=wkv_scales[:],
+                    start=True,
+                    stop=True,
+                )
+            kv_psum_of[g] = kv_psum
 
-        def store_kv(s):
-            if s % PAIR == 0:
-                kv_sb = kv_pool.tile([P, 2, PAIR, KV], F32)
-                kv_of[s // PAIR] = kv_sb
+        def store_kv(g):
+            n = len(GROUPS[g])
+            kv_sb = kv_pool.tile([P, 2, 2, KV], F32)
             nc.scalar.copy(
-                out=kv_of[s // PAIR][:, :, s % PAIR, :],
-                in_=kv_psum_of[s][:].rearrange("p (o d) -> p o d", o=2),
+                out=kv_sb[:, :, :n, :].rearrange("p o i d -> p i o d"),
+                in_=kv_psum_of[g][:, :n, :].rearrange("p i (o d) -> p i o d", o=2),
             )
-            if s % PAIR == PAIR - 1:
-                nc.sync.dma_start(out=pair_view(k_rows, s - (PAIR - 1)), in_=kv_of[s // PAIR][:, 0])
-                nc.sync.dma_start(out=pair_view(v_rows, s - (PAIR - 1)), in_=kv_of[s // PAIR][:, 1])
+            nc.sync.dma_start(out=group_view(k_rows, GROUPS[g]), in_=kv_sb[:, 0, :n, :])
+            nc.sync.dma_start(out=group_view(v_rows, GROUPS[g]), in_=kv_sb[:, 1, :n, :])
 
-        def run(stage, s):
-            if 0 <= s < TILES:
-                stage(s)
+        def run(stage, g, *which):
+            if 0 <= g < len(GROUPS):
+                stage(g, *which)
 
         def step(t):
-            run(transpose_h, t - 3)
-            run(transpose_a, t + 5)
-            run(add_residual, t)
-            run(inverse_rms, t)
-            run(quantise_h, t - 5)
-            run(normalise, t - 2)
-            run(group_a, t + 4)
-            run(group_h, t - 3)
-            run(store_kv, t - 6)
-            run(project_kv, t - 5)
-            run(quantise_a, t + 2)
-            run(project_down, t + 2)
+            run(transpose_h, t - 2)
+            run(transpose_a, t + 2)
+            run(add_residual, t + 0, 0)
+            run(add_residual, t + 0, 1)
+            run(store_kv, t - 4)
+            run(sum_squares, t + 0, 0)
+            run(sum_squares, t + 0, 1)
+            run(inverse_rms, t + 0)
+            run(group_a, t + 2, 0)
+            run(group_a, t + 2, 1)
+            run(group_h, t - 2)
+            run(quantise_h, t - 3)
+            run(quantise_a, t + 1)
+            run(normalise, t - 1, 0)
+            run(normalise, t - 1, 1)
+            run(project_kv, t - 3)
+            run(project_down, t + 1)
 
-        for t in range(-5, 1):
+        for t in range(-2, 0):
             step(t)
         prepare_norm_and_kv()
-        for t in range(1, TILES + 6):
+        for t in range(0, len(GROUPS) + 5):
             step(t)

@@ -25,7 +25,8 @@ DOWN_PASSES = FFN // K_PASS
 TILES = TOKENS // P
 CHUNK_TILES = 4
 CHUNK = CHUNK_TILES * P
-GROUPS = [[s, s + 1] for s in range(0, TILES, 2)]
+GROUPS = [[0], [1]] + [[s, s + 1] for s in range(2, TILES - 2, 2)] + [[TILES - 2], [TILES - 1]]
+GROUP_OF = {s: (g, i) for g, tiles in enumerate(GROUPS) for i, s in enumerate(tiles)}
 
 FLOPS = 2 * TOKENS * FFN * E + 2 * TOKENS * E * (2 * KV)
 
@@ -50,16 +51,16 @@ def tile_textencoderblock_pc_t_kernel(
     with ExitStack() as ctx:
         consts = ctx.enter_context(tc.tile_pool(name="consts", bufs=1))
         a_pool = ctx.enter_context(tc.tile_pool(name="a", bufs=TILES))
-        res_pool = ctx.enter_context(tc.tile_pool(name="res", bufs=TILES // CHUNK_TILES))
-        grouped_pool = ctx.enter_context(tc.tile_pool(name="grouped", bufs=3))
-        mx_pool = ctx.enter_context(tc.tile_pool(name="mx", bufs=2))
+        res_pool = ctx.enter_context(tc.tile_pool(name="res", bufs=14))
+        grouped_pool = ctx.enter_context(tc.tile_pool(name="grouped", bufs=5))
+        mx_pool = ctx.enter_context(tc.tile_pool(name="mx", bufs=3))
         x_pool = ctx.enter_context(tc.tile_pool(name="x", bufs=10))
         stat_pool = ctx.enter_context(tc.tile_pool(name="stat", bufs=4))
-        square_pool = ctx.enter_context(tc.tile_pool(name="square", bufs=4))
+        square_pool = ctx.enter_context(tc.tile_pool(name="square", bufs=2))
         h_pool = ctx.enter_context(tc.tile_pool(name="h", bufs=3))
-        kv_pool = ctx.enter_context(tc.tile_pool(name="kv", bufs=10))
+        kv_pool = ctx.enter_context(tc.tile_pool(name="kv", bufs=8))
         psum_gain = ctx.enter_context(tc.psum_pool(name="psum_gain", bufs=1))
-        psum_a = ctx.enter_context(tc.psum_pool(name="psum_a", bufs=2))
+        psum_a = ctx.enter_context(tc.psum_pool(name="psum_a", bufs=3))
         psum_x = ctx.enter_context(tc.psum_pool(name="psum_x", bufs=2))
         psum_h = ctx.enter_context(tc.psum_pool(name="psum_h", bufs=1))
         psum_kv = ctx.enter_context(tc.psum_pool(name="psum_kv", bufs=1))
@@ -82,42 +83,66 @@ def tile_textencoderblock_pc_t_kernel(
         def load_weight_pass(rows, raw):
             nc.sync.dma_start(out=raw, in_=rows.rearrange("(p t) n -> p t n", t=PACK))
 
-        def load_chunk(c):
-            for j in range(CHUNK_TILES):
-                a_sb = a_pool.tile([P, FFN], BF16)
-                nc.sync.dma_start(out=a_sb[:], in_=chunk_view(a_rows, c)[:, j, :])
-                a_of[c * CHUNK_TILES + j] = a_sb
-            res_sb = res_pool.tile([P, CHUNK_TILES, E], BF16)
-            nc.sync.dma_start(out=res_sb[:], in_=chunk_view(res_rows, c))
-            res_of[c] = res_sb
+        def load_a(s):
+            a_sb = a_pool.tile([P, FFN], BF16)
+            nc.sync.dma_start(out=a_sb[:], in_=chunk_view(a_rows, s // CHUNK_TILES)[:, s % CHUNK_TILES, :])
+            a_of[s] = a_sb
 
-        wd_raw = consts.tile([P, DOWN_PASSES, PACK, E], BF16)
+        def load_res(q):
+            res_sb = res_pool.tile([P, 2, E], BF16)
+            nc.sync.dma_start(out=res_sb[:], in_=group_view(res_rows, [2 * q, 2 * q + 1]))
+            res_of[q] = res_sb
+
+        HALF = E // 2
+        wd_raw = consts.tile([P, DOWN_PASSES, 2, PACK, HALF], BF16)
         wkv_raw = consts.tile([P, 2, PACK, KV], BF16)
-        for g in range(DOWN_PASSES):
-            load_weight_pass(wd[g * K_PASS : (g + 1) * K_PASS, :], wd_raw[:, g])
-        load_chunk(0)
-        nc.sync.dma_start(out=gain_row[0:1, :], in_=ln1_w.unsqueeze(0))
-        load_weight_pass(wk, wkv_raw[:, 0])
-        load_weight_pass(wv, wkv_raw[:, 1])
-        for c in range(1, TILES // CHUNK_TILES):
-            load_chunk(c)
 
-        def group_weight(raw, grouped):
-            nc.vector.tensor_copy(
-                out=grouped.rearrange("p (c i) t -> p c t i", i=4),
-                in_=raw.rearrange("p t (c i) -> p c t i", i=4),
+        def load_wd(k, half):
+            load_weight_pass(
+                wd[k * K_PASS : (k + 1) * K_PASS, half * HALF : (half + 1) * HALF], wd_raw[:, k, half]
             )
+
+        def load_wkv():
+            load_weight_pass(wk, wkv_raw[:, 0])
+            load_weight_pass(wv, wkv_raw[:, 1])
+
+        nc.scalar.dma_start(out=gain_row[0:1, :], in_=ln1_w.unsqueeze(0))
+        load_wd(0, 0)
+        load_wd(0, 1)
+        load_a(0)
+        load_wd(1, 0)
+        load_wd(1, 1)
+        load_a(1)
+        load_a(2)
+        load_a(3)
+        load_res(0)
+        load_a(4)
+        load_a(5)
+        load_a(6)
+        load_a(7)
+        load_wkv()
+        for s in range(8, TILES):
+            load_a(s)
+            if s % 2 == 1 and (s - 8) // 2 + 1 < TILES // 2:
+                load_res((s - 8) // 2 + 1)
+        for q in range(13, TILES // 2):
+            load_res(q)
 
         wd_grouped = consts.tile([P, DOWN_PASSES, E, PACK], BF16, align_bytes=64)
         wd_codes = consts.tile([P, DOWN_PASSES, E], U32, align_bytes=64)
         wd_scales = consts.tile([P, DOWN_PASSES, E], U8, align_bytes=64)
-        for g in range(DOWN_PASSES):
-            group_weight(wd_raw[:, g], wd_grouped[:, g])
-        for g in range(DOWN_PASSES):
+
+        def group_wd(copy, k, half):
+            copy(
+                out=wd_grouped[:, k, half * HALF : (half + 1) * HALF, :].rearrange("p (c i) t -> p c t i", i=4),
+                in_=wd_raw[:, k, half].rearrange("p t (c i) -> p c t i", i=4),
+            )
+
+        def quantise_wd(k):
             nc.vector.quantize_mx(
-                out=wd_codes[:, g, :].bitcast(FP8X4),
-                scales=wd_scales[:, g, :],
-                in_=wd_grouped[:, g].rearrange("p n t -> p (n t)"),
+                out=wd_codes[:, k, :].bitcast(FP8X4),
+                scales=wd_scales[:, k, :],
+                in_=wd_grouped[:, k].rearrange("p n t -> p (n t)"),
             )
 
         wkv_grouped = consts.tile([P, 2, KV, PACK], BF16, align_bytes=64)
@@ -125,9 +150,10 @@ def tile_textencoderblock_pc_t_kernel(
         wkv_scales = consts.tile([P, 2 * KV], U8, align_bytes=64)
 
         gain = psum_gain.tile([P, E], F32)
+        nc.tensor.matmul(out=gain[:], lhsT=ones[:], rhs=gain_row[:], start=True, stop=True)
+
 
         def prepare_norm_and_kv():
-            nc.tensor.matmul(out=gain[:], lhsT=ones[:], rhs=gain_row[:], start=True, stop=True)
             for s in range(2):
                 nc.vector.tensor_copy(
                     out=wkv_grouped[:, s].rearrange("p n (u e) -> p n u e", u=2),
@@ -139,25 +165,23 @@ def tile_textencoderblock_pc_t_kernel(
                 in_=wkv_grouped[:].rearrange("p s n t -> p (s n t)"),
             )
 
-        def transpose_a(g):
-            for s in GROUPS[g]:
-                a_words = a_of[s][:].bitcast(F32)
-                aT = psum_a.tile([P, PACK * P], F32)
-                for ku in range(PACK):
-                    k, u = divmod(ku, 2)
-                    words = slice(2 * P * k + u, 2 * P * (k + 1), 2)
-                    nc.tensor.transpose(aT[:, ku * P : (ku + 1) * P], a_words[:, words], ident[:])
-                aT_of[s] = aT
+        def transpose_a(s):
+            a_words = a_of[s][:].bitcast(F32)
+            aT = psum_a.tile([P, PACK * P], F32)
+            for ku in range(PACK):
+                k, u = divmod(ku, 2)
+                words = slice(2 * P * k + u, 2 * P * (k + 1), 2)
+                nc.tensor.transpose(aT[:, ku * P : (ku + 1) * P], a_words[:, words], ident[:])
+            aT_of[s] = aT
 
-        def group_a(g, i):
-            if i >= len(GROUPS[g]):
-                return
+        def group_a(s):
+            g, i = GROUP_OF[s]
             if i == 0:
                 a_grouped = grouped_pool.tile([P, 2, FFN], BF16, align_bytes=64)
                 a_grouped_of[g] = a_grouped
             nc.scalar.copy(
                 out=a_grouped_of[g][:, i, :].bitcast(F32).rearrange("p (g r u) -> p g r u", g=DOWN_PASSES, u=2),
-                in_=aT_of[GROUPS[g][i]][:].rearrange("p (g u r) -> p g r u", g=DOWN_PASSES, u=2),
+                in_=aT_of[s][:].rearrange("p (g u r) -> p g r u", g=DOWN_PASSES, u=2),
             )
 
         def quantise_a(g):
@@ -199,7 +223,7 @@ def tile_textencoderblock_pc_t_kernel(
             nc.vector.tensor_tensor(
                 out=x_of[g][:, i, :],
                 in0=x_psum_of[s][:],
-                in1=res_of[s // CHUNK_TILES][:, s % CHUNK_TILES, :],
+                in1=res_of[s // 2][:, s % 2, :],
                 op=ALU.add,
             )
             if i == n - 1:
@@ -229,7 +253,7 @@ def tile_textencoderblock_pc_t_kernel(
         def normalise(g, i):
             if i >= len(GROUPS[g]):
                 return
-            if i == 0:
+            if g not in h_of:
                 h_sb = h_pool.tile([P, 2, E], BF16)
                 h_of[g] = h_sb
             nc.vector.scalar_tensor_tensor(
@@ -300,27 +324,48 @@ def tile_textencoderblock_pc_t_kernel(
             if 0 <= g < len(GROUPS):
                 stage(g, *which)
 
-        def step(t):
-            run(transpose_h, t - 2)
-            run(transpose_a, t + 2)
-            run(add_residual, t + 0, 0)
-            run(add_residual, t + 0, 1)
-            run(store_kv, t - 4)
-            run(sum_squares, t + 0, 0)
-            run(sum_squares, t + 0, 1)
-            run(inverse_rms, t + 0)
-            run(group_a, t + 2, 0)
-            run(group_a, t + 2, 1)
-            run(group_h, t - 2)
-            run(quantise_h, t - 3)
-            run(quantise_a, t + 1)
-            run(normalise, t - 1, 0)
-            run(normalise, t - 1, 1)
-            run(project_kv, t - 3)
-            run(project_down, t + 1)
+        def a_upto(t):
+            return min(TILES, 7 + 1 * GROUPS[min(t, len(GROUPS) - 1)][-1] // 1) if t >= 0 else 4
 
-        for t in range(-2, 0):
+        def step(t):
+            tiles = range(a_upto(t - 1), a_upto(t))
+            run(transpose_h, t - 3)
+            for s in tiles:
+                transpose_a(s)
+            run(add_residual, t, 0)
+            run(add_residual, t, 1)
+            run(store_kv, t - 5)
+            run(group_h, t - 3)
+            run(sum_squares, t, 0)
+            run(sum_squares, t, 1)
+            run(inverse_rms, t)
+            for s in tiles:
+                group_a(s)
+            run(quantise_h, t - 4)
+            run(quantise_a, t + 2)
+            run(normalise, t - 2, 0)
+            run(normalise, t - 2, 1)
+            run(project_down, t + 1)
+            run(project_kv, t - 4)
+
+        group_wd(nc.vector.tensor_copy, 0, 0)
+        group_wd(nc.vector.tensor_copy, 0, 1)
+        quantise_wd(0)
+        group_wd(nc.vector.tensor_copy, 1, 0)
+        group_wd(nc.vector.tensor_copy, 1, 1)
+        for s in range(a_upto(-1)):
+            transpose_a(s)
+            group_a(s)
+            if s == 0:
+                quantise_a(0)
+                quantise_wd(1)
+            if s == 3:
+                project_down(0)
+            if s == 1:
+                quantise_a(1)
+            if s == 1 and False:
+                prepare_norm_and_kv()
+        for t in range(0, len(GROUPS) + 6):
             step(t)
-        prepare_norm_and_kv()
-        for t in range(0, len(GROUPS) + 5):
-            step(t)
+            if t == 0:
+                prepare_norm_and_kv()

@@ -103,10 +103,10 @@ def tile_textencoderblock_pc_t_kernel(
             )
 
         def load_wkv():
+            nc.sync.dma_start(out=gain_row[0:1, :], in_=ln1_w.unsqueeze(0))
             load_weight_pass(wk, wkv_raw[:, 0])
             load_weight_pass(wv, wkv_raw[:, 1])
 
-        nc.scalar.dma_start(out=gain_row[0:1, :], in_=ln1_w.unsqueeze(0))
         load_wd(0, 0)
         load_wd(0, 1)
         load_a(0)
@@ -150,10 +150,9 @@ def tile_textencoderblock_pc_t_kernel(
         wkv_scales = consts.tile([P, 2 * KV], U8, align_bytes=64)
 
         gain = psum_gain.tile([P, E], F32)
-        nc.tensor.matmul(out=gain[:], lhsT=ones[:], rhs=gain_row[:], start=True, stop=True)
-
 
         def prepare_norm_and_kv():
+            nc.tensor.matmul(out=gain[:], lhsT=ones[:], rhs=gain_row[:], start=True, stop=True)
             for s in range(2):
                 nc.vector.tensor_copy(
                     out=wkv_grouped[:, s].rearrange("p n (u e) -> p n u e", u=2),
@@ -325,7 +324,7 @@ def tile_textencoderblock_pc_t_kernel(
                 stage(g, *which)
 
         def a_upto(t):
-            return min(TILES, 7 + 1 * GROUPS[min(t, len(GROUPS) - 1)][-1] // 1) if t >= 0 else 4
+            return min(TILES, 7 + GROUPS[min(t, len(GROUPS) - 1)][-1]) if t >= 0 else 4
 
         def step(t):
             tiles = range(a_upto(t - 1), a_upto(t))
@@ -363,8 +362,6 @@ def tile_textencoderblock_pc_t_kernel(
                 project_down(0)
             if s == 1:
                 quantise_a(1)
-            if s == 1 and False:
-                prepare_norm_and_kv()
         for t in range(0, len(GROUPS) + 6):
             step(t)
             if t == 0:

@@ -71,7 +71,7 @@ def tile_textencoderblock_pc_t_kernel(
 
         ident = consts.tile([P, P], F32)
         make_identity(nc, ident[:])
-        ones = consts.tile([P, P], BF16)
+        ones = consts.tile([P, E], BF16)
         nc.vector.memset(ones[:], 1.0)
         gain_row = consts.tile([P, E], BF16)
         nc.vector.memset(gain_row[:], 0.0)
@@ -151,8 +151,13 @@ def tile_textencoderblock_pc_t_kernel(
 
         gain = psum_gain.tile([P, E], F32)
 
+        def warm_up(n):
+            for i in range(n):
+                nc.tensor.matmul(out=gain[:], lhsT=ones[:, :P], rhs=ones[:], start=True, stop=True)
+
+
         def prepare_norm_and_kv():
-            nc.tensor.matmul(out=gain[:], lhsT=ones[:], rhs=gain_row[:], start=True, stop=True)
+            nc.tensor.matmul(out=gain[:], lhsT=ones[:, :P], rhs=gain_row[:], start=True, stop=True)
             for s in range(2):
                 nc.vector.tensor_copy(
                     out=wkv_grouped[:, s].rearrange("p n (u e) -> p n u e", u=2),
@@ -347,6 +352,7 @@ def tile_textencoderblock_pc_t_kernel(
             run(project_down, t + 1)
             run(project_kv, t - 4)
 
+        warm_up(8)
         group_wd(nc.vector.tensor_copy, 0, 0)
         group_wd(nc.vector.tensor_copy, 0, 1)
         quantise_wd(0)
@@ -354,6 +360,8 @@ def tile_textencoderblock_pc_t_kernel(
         group_wd(nc.vector.tensor_copy, 1, 1)
         for s in range(a_upto(-1)):
             transpose_a(s)
+            if s == 0:
+                warm_up(2)
             group_a(s)
             if s == 0:
                 quantise_a(0)

@@ -25,6 +25,8 @@ DOWN_PASSES = FFN // K_PASS
 TILES = TOKENS // P
 CHUNK_TILES = 4
 CHUNK = CHUNK_TILES * P
+CHUNKS = TOKENS // CHUNK
+SHORT_STORES = CHUNKS - 2
 GROUPS = [[0], [1]] + [[s, s + 1] for s in range(2, TILES - 2, 2)] + [[TILES - 2], [TILES - 1]]
 GROUP_OF = {s: (g, i) for g, tiles in enumerate(GROUPS) for i, s in enumerate(tiles)}
 
@@ -50,15 +52,15 @@ def tile_textencoderblock_pc_t_kernel(
 
     with ExitStack() as ctx:
         consts = ctx.enter_context(tc.tile_pool(name="consts", bufs=1))
-        a_pool = ctx.enter_context(tc.tile_pool(name="a", bufs=TILES))
-        res_pool = ctx.enter_context(tc.tile_pool(name="res", bufs=14))
+        a_pool = ctx.enter_context(tc.tile_pool(name="a", bufs=6))
+        res_pool = ctx.enter_context(tc.tile_pool(name="res", bufs=7))
         grouped_pool = ctx.enter_context(tc.tile_pool(name="grouped", bufs=5))
         mx_pool = ctx.enter_context(tc.tile_pool(name="mx", bufs=3))
-        x_pool = ctx.enter_context(tc.tile_pool(name="x", bufs=10))
+        x_pool = ctx.enter_context(tc.tile_pool(name="x", bufs=5))
         stat_pool = ctx.enter_context(tc.tile_pool(name="stat", bufs=4))
         square_pool = ctx.enter_context(tc.tile_pool(name="square", bufs=2))
         h_pool = ctx.enter_context(tc.tile_pool(name="h", bufs=3))
-        kv_pool = ctx.enter_context(tc.tile_pool(name="kv", bufs=8))
+        kv_pool = ctx.enter_context(tc.tile_pool(name="kv", bufs=6))
         psum_gain = ctx.enter_context(tc.psum_pool(name="psum_gain", bufs=1))
         psum_a = ctx.enter_context(tc.psum_pool(name="psum_a", bufs=3))
         psum_x = ctx.enter_context(tc.psum_pool(name="psum_x", bufs=2))
@@ -67,7 +69,7 @@ def tile_textencoderblock_pc_t_kernel(
         ctx.enter_context(tc.manual_schedule())
 
         a_of, res_of, aT_of, a_grouped_of, a_mx_of, x_psum_of, x_of = {}, {}, {}, {}, {}, {}, {}
-        sum_of, rstd_of, h_of, hT_of, h_grouped_of, h_mx_of, kv_psum_of = {}, {}, {}, {}, {}, {}, {}
+        sum_of, rstd_of, h_of, hT_of, h_grouped_of, h_mx_of, kv_psum_of, kv_of = {}, {}, {}, {}, {}, {}, {}, {}
 
         ident = consts.tile([P, P], F32)
         make_identity(nc, ident[:])
@@ -83,15 +85,18 @@ def tile_textencoderblock_pc_t_kernel(
         def load_weight_pass(rows, raw):
             nc.sync.dma_start(out=raw, in_=rows.rearrange("(p t) n -> p t n", t=PACK))
 
-        def load_a(s):
-            a_sb = a_pool.tile([P, FFN], BF16)
-            nc.sync.dma_start(out=a_sb[:], in_=chunk_view(a_rows, s // CHUNK_TILES)[:, s % CHUNK_TILES, :])
-            a_of[s] = a_sb
+        def load_tiles(rows, pool, width, tile_of, s, n):
+            c, j = divmod(s, CHUNK_TILES)
+            if j == 0:
+                loaded = pool.tile([P, CHUNK_TILES, width], BF16)
+                tile_of[c] = loaded
+            nc.sync.dma_start(out=tile_of[c][:, j : j + n, :], in_=chunk_view(rows, c)[:, j : j + n, :])
 
-        def load_res(q):
-            res_sb = res_pool.tile([P, 2, E], BF16)
-            nc.sync.dma_start(out=res_sb[:], in_=group_view(res_rows, [2 * q, 2 * q + 1]))
-            res_of[q] = res_sb
+        def load_a(s, n=1):
+            load_tiles(a_rows, a_pool, FFN, a_of, s, n)
+
+        def load_res(s, n):
+            load_tiles(res_rows, res_pool, E, res_of, s, n)
 
         HALF = E // 2
         wd_raw = consts.tile([P, DOWN_PASSES, 2, PACK, HALF], BF16)
@@ -115,18 +120,19 @@ def tile_textencoderblock_pc_t_kernel(
         load_a(1)
         load_a(2)
         load_a(3)
-        load_res(0)
+        load_res(0, 2)
         load_a(4)
         load_a(5)
-        load_a(6)
-        load_a(7)
+        load_a(6, 2)
         load_wkv()
-        for s in range(8, TILES):
-            load_a(s)
-            if s % 2 == 1 and (s - 8) // 2 + 1 < TILES // 2:
-                load_res((s - 8) // 2 + 1)
-        for q in range(13, TILES // 2):
-            load_res(q)
+        load_res(2, 2)
+        load_a(8, 2)
+        load_a(10, 2)
+        load_res(4, 4)
+        for c in range(3, CHUNKS):
+            load_a(c * CHUNK_TILES, CHUNK_TILES)
+            load_res((c - 1) * CHUNK_TILES, CHUNK_TILES)
+        load_res((CHUNKS - 1) * CHUNK_TILES, CHUNK_TILES)
 
         wd_grouped = consts.tile([P, DOWN_PASSES, E, PACK], BF16, align_bytes=64)
         wd_codes = consts.tile([P, DOWN_PASSES, E], U32, align_bytes=64)
@@ -170,7 +176,7 @@ def tile_textencoderblock_pc_t_kernel(
             )
 
         def transpose_a(s):
-            a_words = a_of[s][:].bitcast(F32)
+            a_words = a_of[s // CHUNK_TILES][:, s % CHUNK_TILES, :].bitcast(F32)
             aT = psum_a.tile([P, PACK * P], F32)
             for ku in range(PACK):
                 k, u = divmod(ku, 2)
@@ -221,17 +227,20 @@ def tile_textencoderblock_pc_t_kernel(
             if i >= n:
                 return
             s = GROUPS[g][i]
-            if i == 0:
-                x_sb = x_pool.tile([P, 2, E], F32)
-                x_of[g] = x_sb
+            c, j = divmod(s, CHUNK_TILES)
+            if j == 0:
+                x_sb = x_pool.tile([P, CHUNK_TILES, E], F32)
+                x_of[c] = x_sb
             nc.vector.tensor_tensor(
-                out=x_of[g][:, i, :],
+                out=x_of[c][:, j, :],
                 in0=x_psum_of[s][:],
-                in1=res_of[s // 2][:, s % 2, :],
+                in1=res_of[c][:, j, :],
                 op=ALU.add,
             )
-            if i == n - 1:
-                nc.sync.dma_start(out=group_view(x_rows, GROUPS[g]), in_=x_of[g][:, :n, :])
+            if c >= SHORT_STORES and i == n - 1:
+                nc.sync.dma_start(out=group_view(x_rows, GROUPS[g]), in_=x_of[c][:, j - n + 1 : j + 1, :])
+            elif c < SHORT_STORES and j == CHUNK_TILES - 1:
+                nc.sync.dma_start(out=chunk_view(x_rows, c), in_=x_of[c][:])
 
         def sum_squares(g, i):
             if i >= len(GROUPS[g]):
@@ -240,8 +249,9 @@ def tile_textencoderblock_pc_t_kernel(
                 sum_sq = stat_pool.tile([P, 2], F32)
                 sum_of[g] = sum_sq
             squares = square_pool.tile([P, E], BF16)
+            c, j = divmod(GROUPS[g][i], CHUNK_TILES)
             nc.scalar.activation(
-                out=squares[:], in_=x_of[g][:, i, :], func=ACT.Square, accum_out=sum_of[g][:, i : i + 1]
+                out=squares[:], in_=x_of[c][:, j, :], func=ACT.Square, accum_out=sum_of[g][:, i : i + 1]
             )
 
         def inverse_rms(g):
@@ -260,9 +270,10 @@ def tile_textencoderblock_pc_t_kernel(
             if g not in h_of:
                 h_sb = h_pool.tile([P, 2, E], BF16)
                 h_of[g] = h_sb
+            c, j = divmod(GROUPS[g][i], CHUNK_TILES)
             nc.vector.scalar_tensor_tensor(
                 out=h_of[g][:, i, :].rearrange("p (u j) -> p u j", u=2),
-                in0=x_of[g][:, i, :].rearrange("p (j u) -> p u j", u=2),
+                in0=x_of[c][:, j, :].rearrange("p (j u) -> p u j", u=2),
                 scalar=rstd_of[g][:, i : i + 1],
                 in1=gain[:].rearrange("p (j u) -> p u j", u=2),
                 op0=ALU.mult,
@@ -316,13 +327,19 @@ def tile_textencoderblock_pc_t_kernel(
 
         def store_kv(g):
             n = len(GROUPS[g])
-            kv_sb = kv_pool.tile([P, 2, 2, KV], F32)
+            c, j = divmod(GROUPS[g][0], CHUNK_TILES)
+            if j == 0:
+                kv_sb = kv_pool.tile([P, 2, CHUNK_TILES, KV], F32)
+                kv_of[c] = kv_sb
             nc.scalar.copy(
-                out=kv_sb[:, :, :n, :].rearrange("p o i d -> p i o d"),
+                out=kv_of[c][:, :, j : j + n, :].rearrange("p o i d -> p i o d"),
                 in_=kv_psum_of[g][:, :n, :].rearrange("p i (o d) -> p i o d", o=2),
             )
-            nc.sync.dma_start(out=group_view(k_rows, GROUPS[g]), in_=kv_sb[:, 0, :n, :])
-            nc.sync.dma_start(out=group_view(v_rows, GROUPS[g]), in_=kv_sb[:, 1, :n, :])
+            for o, rows in enumerate((k_rows, v_rows)):
+                if c >= SHORT_STORES:
+                    nc.sync.dma_start(out=group_view(rows, GROUPS[g]), in_=kv_of[c][:, o, j : j + n, :])
+                elif j + n == CHUNK_TILES:
+                    nc.sync.dma_start(out=chunk_view(rows, c), in_=kv_of[c][:, o])
 
         def run(stage, g, *which):
             if 0 <= g < len(GROUPS):

@@ -58,7 +58,7 @@ def tile_textencoderblock_pc_t_kernel(
         mx_pool = ctx.enter_context(tc.tile_pool(name="mx", bufs=3))
         x_pool = ctx.enter_context(tc.tile_pool(name="x", bufs=5))
         stat_pool = ctx.enter_context(tc.tile_pool(name="stat", bufs=4))
-        square_pool = ctx.enter_context(tc.tile_pool(name="square", bufs=2))
+        square_pool = ctx.enter_context(tc.tile_pool(name="square", bufs=4))
         h_pool = ctx.enter_context(tc.tile_pool(name="h", bufs=3))
         kv_pool = ctx.enter_context(tc.tile_pool(name="kv", bufs=6))
         psum_gain = ctx.enter_context(tc.psum_pool(name="psum_gain", bufs=1))

@@ -77,10 +77,10 @@ def tile_textencoderblock_pc_t_kernel(
         nc.vector.memset(ones[:], 1.0)
         gain_row = consts.tile([P, E], BF16)
         nc.vector.memset(gain_row[:], 0.0)
-        minus_half = consts.tile([P, 2], F32)
-        nc.vector.memset(minus_half[:], -0.5)
+        eps = consts.tile([P, 1], F32)
+        nc.vector.memset(eps[:], EPS)
         table_warmer = consts.tile([P, 1], F32)
-        nc.scalar.activation(out=table_warmer[:], in_=minus_half[:, 0:1], func=ACT.Square)
+        nc.scalar.activation(out=table_warmer[:], in_=eps[:], func=ACT.Abs_reciprocal_sqrt)
 
         def load_weight_pass(rows, raw):
             nc.sync.dma_start(out=raw, in_=rows.rearrange("(p t) n -> p t n", t=PACK))
@@ -256,12 +256,10 @@ def tile_textencoderblock_pc_t_kernel(
 
         def inverse_rms(g):
             n = len(GROUPS[g])
-            mean_sq = stat_pool.tile([P, 2], F32)
-            nc.gpsimd.tensor_scalar(
-                out=mean_sq[:, :n], in0=sum_of[g][:, :n], scalar1=1.0 / E, scalar2=EPS, op0=ALU.mult, op1=ALU.add
-            )
             rstd = stat_pool.tile([P, 2], F32)
-            nc.gpsimd.tensor_tensor(out=rstd[:, :n], in0=mean_sq[:, :n], in1=minus_half[:, :n], op=ALU.pow)
+            nc.scalar.activation(
+                out=rstd[:, :n], in_=sum_of[g][:, :n], func=ACT.Abs_reciprocal_sqrt, scale=1.0 / E, bias=eps[:]
+            )
             rstd_of[g] = rstd
 
         def normalise(g, i):
@@ -359,9 +357,9 @@ def tile_textencoderblock_pc_t_kernel(
             run(group_h, t - 3)
             run(sum_squares, t, 0)
             run(sum_squares, t, 1)
-            run(inverse_rms, t)
             for s in tiles:
                 group_a(s)
+            run(inverse_rms, t)
             run(quantise_h, t - 4)
             run(quantise_a, t + 2)
             run(normalise, t - 2, 0)

@@ -61,11 +61,10 @@ def tile_textencoderblock_pc_t_kernel(
         square_pool = ctx.enter_context(tc.tile_pool(name="square", bufs=4))
         h_pool = ctx.enter_context(tc.tile_pool(name="h", bufs=3))
         kv_pool = ctx.enter_context(tc.tile_pool(name="kv", bufs=6))
-        psum_gain = ctx.enter_context(tc.psum_pool(name="psum_gain", bufs=1))
         psum_a = ctx.enter_context(tc.psum_pool(name="psum_a", bufs=3))
         psum_x = ctx.enter_context(tc.psum_pool(name="psum_x", bufs=2))
         psum_h = ctx.enter_context(tc.psum_pool(name="psum_h", bufs=1))
-        psum_kv = ctx.enter_context(tc.psum_pool(name="psum_kv", bufs=1))
+        psum_kv = ctx.enter_context(tc.psum_pool(name="psum_kv", bufs=2))
         ctx.enter_context(tc.manual_schedule())
 
         a_of, res_of, aT_of, a_grouped_of, a_mx_of, x_psum_of, x_of = {}, {}, {}, {}, {}, {}, {}
@@ -155,15 +154,17 @@ def tile_textencoderblock_pc_t_kernel(
         wkv_codes = consts.tile([P, 2 * KV], U32, align_bytes=64)
         wkv_scales = consts.tile([P, 2 * KV], U8, align_bytes=64)
 
-        gain = psum_gain.tile([P, E], F32)
+        gain = consts.tile([P, E], F32)
+        spare = psum_kv.tile([P, E], F32, name="kv_psum")
 
         def warm_up(n):
             for i in range(n):
-                nc.tensor.matmul(out=gain[:], lhsT=ones[:, :P], rhs=ones[:], start=True, stop=True)
+                nc.tensor.matmul(out=spare[:], lhsT=ones[:, :P], rhs=ones[:], start=True, stop=True)
 
 
         def prepare_norm_and_kv():
-            nc.tensor.matmul(out=gain[:], lhsT=ones[:, :P], rhs=gain_row[:], start=True, stop=True)
+            nc.tensor.matmul(out=spare[:], lhsT=ones[:, :P], rhs=gain_row[:], start=True, stop=True)
+            nc.scalar.copy(out=gain[:], in_=spare[:])
             for s in range(2):
                 nc.vector.tensor_copy(
                     out=wkv_grouped[:, s].rearrange("p n (u e) -> p n u e", u=2),
@@ -348,24 +349,24 @@ def tile_textencoderblock_pc_t_kernel(
 
         def step(t):
             tiles = range(a_upto(t - 1), a_upto(t))
-            run(transpose_h, t - 3)
+            run(transpose_h, t - 2)
             for s in tiles:
                 transpose_a(s)
             run(add_residual, t, 0)
             run(add_residual, t, 1)
-            run(store_kv, t - 5)
-            run(group_h, t - 3)
+            run(store_kv, t - 4)
+            run(group_h, t - 2)
             run(sum_squares, t, 0)
             run(sum_squares, t, 1)
             for s in tiles:
                 group_a(s)
             run(inverse_rms, t)
-            run(quantise_h, t - 4)
             run(quantise_a, t + 2)
-            run(normalise, t - 2, 0)
-            run(normalise, t - 2, 1)
+            run(normalise, t - 1, 0)
+            run(normalise, t - 1, 1)
+            run(quantise_h, t - 2)
             run(project_down, t + 1)
-            run(project_kv, t - 4)
+            run(project_kv, t - 3)
 
         warm_up(8)
         group_wd(nc.vector.tensor_copy, 0, 0)
@@ -385,7 +386,7 @@ def tile_textencoderblock_pc_t_kernel(
                 project_down(0)
             if s == 1:
                 quantise_a(1)
-        for t in range(0, len(GROUPS) + 6):
+        for t in range(0, len(GROUPS) + 5):
             step(t)
             if t == 0:
                 prepare_norm_and_kv()

from contextlib import ExitStack

import concourse.mybir as mybir
from concourse.masks import make_identity

F32 = mybir.dt.float32
BF16 = mybir.dt.bfloat16
U32 = mybir.dt.uint32
U8 = mybir.dt.uint8
FP8X4 = mybir.dt.float8_e4m3fn_x4
ACT = mybir.ActivationFunctionType
ALU = mybir.AluOpType

P = 128
PACK = 4
K_PASS = P * PACK

TOKENS = 4096
FFN = 1024
E = 512
KV = 128
EPS = 2.0**-23
DOWN_PASSES = FFN // K_PASS

TILES = TOKENS // P
CHUNK_TILES = 4
CHUNK = CHUNK_TILES * P
CHUNKS = TOKENS // CHUNK
SHORT_STORES = CHUNKS - 2
GROUPS = [[0], [1]] + [[s, s + 1] for s in range(2, TILES - 2, 2)] + [[TILES - 2], [TILES - 1]]
GROUP_OF = {s: (g, i) for g, tiles in enumerate(GROUPS) for i, s in enumerate(tiles)}

FLOPS = 2 * TOKENS * FFN * E + 2 * TOKENS * E * (2 * KV)


def tile_textencoderblock_pc_t_kernel(
    tc, ffn_act, wd, residual, ln1_w, wk, wv, out_0, out_1, out_2
):
    nc = tc.nc
    a_rows = ffn_act.flatten_outer_dims()
    res_rows = residual.flatten_outer_dims()
    x_rows = out_0.flatten_outer_dims()
    k_rows = out_1.flatten_outer_dims()
    v_rows = out_2.flatten_outer_dims()

    def chunk_view(rows, c):
        return rows[c * CHUNK : (c + 1) * CHUNK, :].rearrange("(p j) w -> p j w", j=CHUNK_TILES)

    def group_view(rows, tiles):
        j0 = tiles[0] % CHUNK_TILES
        return chunk_view(rows, tiles[0] // CHUNK_TILES)[:, j0 : j0 + len(tiles), :]

    with ExitStack() as ctx:
        consts = ctx.enter_context(tc.tile_pool(name="consts", bufs=1))
        a_pool = ctx.enter_context(tc.tile_pool(name="a", bufs=6))
        res_pool = ctx.enter_context(tc.tile_pool(name="res", bufs=7))
        grouped_pool = ctx.enter_context(tc.tile_pool(name="grouped", bufs=5))
        mx_pool = ctx.enter_context(tc.tile_pool(name="mx", bufs=3))
        x_pool = ctx.enter_context(tc.tile_pool(name="x", bufs=5))
        stat_pool = ctx.enter_context(tc.tile_pool(name="stat", bufs=4))
        square_pool = ctx.enter_context(tc.tile_pool(name="square", bufs=4))
        h_pool = ctx.enter_context(tc.tile_pool(name="h", bufs=3))
        kv_pool = ctx.enter_context(tc.tile_pool(name="kv", bufs=6))
        psum_a = ctx.enter_context(tc.psum_pool(name="psum_a", bufs=3))
        psum_x = ctx.enter_context(tc.psum_pool(name="psum_x", bufs=2))
        psum_h = ctx.enter_context(tc.psum_pool(name="psum_h", bufs=1))
        psum_kv = ctx.enter_context(tc.psum_pool(name="psum_kv", bufs=2))
        ctx.enter_context(tc.manual_schedule())

        a_of, res_of, aT_of, a_grouped_of, a_mx_of, x_psum_of, x_of = {}, {}, {}, {}, {}, {}, {}
        sum_of, rstd_of, h_of, hT_of, h_grouped_of, h_mx_of, kv_psum_of, kv_of = {}, {}, {}, {}, {}, {}, {}, {}

        ident = consts.tile([P, P], F32)
        make_identity(nc, ident[:])
        ones = consts.tile([P, E], BF16)
        nc.vector.memset(ones[:], 1.0)
        gain_row = consts.tile([P, E], BF16)
        nc.vector.memset(gain_row[:], 0.0)
        eps = consts.tile([P, 1], F32)
        nc.vector.memset(eps[:], EPS)
        table_warmer = consts.tile([P, 1], F32)
        nc.scalar.activation(out=table_warmer[:], in_=eps[:], func=ACT.Abs_reciprocal_sqrt)

        def load_weight_pass(rows, raw):
            nc.sync.dma_start(out=raw, in_=rows.rearrange("(p t) n -> p t n", t=PACK))

        def load_tiles(rows, pool, width, tile_of, s, n):
            c, j = divmod(s, CHUNK_TILES)
            if j == 0:
                loaded = pool.tile([P, CHUNK_TILES, width], BF16)
                tile_of[c] = loaded
            nc.sync.dma_start(out=tile_of[c][:, j : j + n, :], in_=chunk_view(rows, c)[:, j : j + n, :])

        def load_a(s, n=1):
            load_tiles(a_rows, a_pool, FFN, a_of, s, n)

        def load_res(s, n):
            load_tiles(res_rows, res_pool, E, res_of, s, n)

        HALF = E // 2
        wd_raw = consts.tile([P, DOWN_PASSES, 2, PACK, HALF], BF16)
        wkv_raw = consts.tile([P, 2, PACK, KV], BF16)

        def load_wd(k, half):
            load_weight_pass(
                wd[k * K_PASS : (k + 1) * K_PASS, half * HALF : (half + 1) * HALF], wd_raw[:, k, half]
            )

        def load_wkv():
            nc.sync.dma_start(out=gain_row[0:1, :], in_=ln1_w.unsqueeze(0))
            load_weight_pass(wk, wkv_raw[:, 0])
            load_weight_pass(wv, wkv_raw[:, 1])

        load_wd(0, 0)
        load_wd(0, 1)
        load_a(0)
        load_wd(1, 0)
        load_wd(1, 1)
        load_a(1)
        load_a(2)
        load_a(3)
        load_res(0, 2)
        load_a(4)
        load_a(5)
        load_a(6, 2)
        load_wkv()
        load_res(2, 2)
        load_a(8, 2)
        load_a(10, 2)
        load_res(4, 4)
        for c in range(3, CHUNKS):
            load_a(c * CHUNK_TILES, CHUNK_TILES)
            load_res((c - 1) * CHUNK_TILES, CHUNK_TILES)
        load_res((CHUNKS - 1) * CHUNK_TILES, CHUNK_TILES)

        wd_grouped = consts.tile([P, DOWN_PASSES, E, PACK], BF16, align_bytes=64)
        wd_codes = consts.tile([P, DOWN_PASSES, E], U32, align_bytes=64)
        wd_scales = consts.tile([P, DOWN_PASSES, E], U8, align_bytes=64)

        def group_wd(copy, k, half):
            copy(
                out=wd_grouped[:, k, half * HALF : (half + 1) * HALF, :].rearrange("p (c i) t -> p c t i", i=4),
                in_=wd_raw[:, k, half].rearrange("p t (c i) -> p c t i", i=4),
            )

        def quantise_wd(k):
            nc.vector.quantize_mx(
                out=wd_codes[:, k, :].bitcast(FP8X4),
                scales=wd_scales[:, k, :],
                in_=wd_grouped[:, k].rearrange("p n t -> p (n t)"),
            )

        wkv_grouped = consts.tile([P, 2, KV, PACK], BF16, align_bytes=64)
        wkv_codes = consts.tile([P, 2 * KV], U32, align_bytes=64)
        wkv_scales = consts.tile([P, 2 * KV], U8, align_bytes=64)

        gain = consts.tile([P, E], F32)
        spare = psum_kv.tile([P, E], F32, name="kv_psum")

        def warm_up(n):
            for i in range(n):
                nc.tensor.matmul(out=spare[:], lhsT=ones[:, :P], rhs=ones[:], start=True, stop=True)


        def prepare_norm_and_kv():
            nc.tensor.matmul(out=spare[:], lhsT=ones[:, :P], rhs=gain_row[:], start=True, stop=True)
            nc.scalar.copy(out=gain[:], in_=spare[:])
            for s in range(2):
                nc.vector.tensor_copy(
                    out=wkv_grouped[:, s].rearrange("p n (u e) -> p n u e", u=2),
                    in_=wkv_raw[:, s].rearrange("p (e u) n -> p n u e", u=2),
                )
            nc.vector.quantize_mx(
                out=wkv_codes[:].bitcast(FP8X4),
                scales=wkv_scales[:],
                in_=wkv_grouped[:].rearrange("p s n t -> p (s n t)"),
            )

        def transpose_a(s):
            a_words = a_of[s // CHUNK_TILES][:, s % CHUNK_TILES, :].bitcast(F32)
            aT = psum_a.tile([P, PACK * P], F32)
            for ku in range(PACK):
                k, u = divmod(ku, 2)
                words = slice(2 * P * k + u, 2 * P * (k + 1), 2)
                nc.tensor.transpose(aT[:, ku * P : (ku + 1) * P], a_words[:, words], ident[:])
            aT_of[s] = aT

        def group_a(s):
            g, i = GROUP_OF[s]
            if i == 0:
                a_grouped = grouped_pool.tile([P, 2, FFN], BF16, align_bytes=64)
                a_grouped_of[g] = a_grouped
            nc.scalar.copy(
                out=a_grouped_of[g][:, i, :].bitcast(F32).rearrange("p (g r u) -> p g r u", g=DOWN_PASSES, u=2),
                in_=aT_of[s][:].rearrange("p (g u r) -> p g r u", g=DOWN_PASSES, u=2),
            )

        def quantise_a(g):
            n = len(GROUPS[g])
            a_codes = mx_pool.tile([P, 2 * DOWN_PASSES * P], U32, align_bytes=64)
            a_scales = mx_pool.tile([P, 2 * DOWN_PASSES * P], U8, align_bytes=64)
            nc.vector.quantize_mx(
                out=a_codes[:, : n * DOWN_PASSES * P].bitcast(FP8X4),
                scales=a_scales[:, : n * DOWN_PASSES * P],
                in_=a_grouped_of[g][:].rearrange("p i k -> p (i k)")[:, : n * FFN],
            )
            a_mx_of[g] = (a_codes, a_scales)

        def project_down(g):
            a_codes, a_scales = a_mx_of[g]
            for i, s in enumerate(GROUPS[g]):
                x_psum = psum_x.tile([P, E], F32)
                for k in range(DOWN_PASSES):
                    cols = slice((i * DOWN_PASSES + k) * P, (i * DOWN_PASSES + k + 1) * P)
                    nc.tensor.matmul_mx(
                        out=x_psum[:],
                        lhsT=a_codes[:, cols].bitcast(FP8X4),
                        lhsT_scale=a_scales[:, cols],
                        rhs=wd_codes[:, k, :].bitcast(FP8X4),
                        rhs_scale=wd_scales[:, k, :],
                        start=(k == 0),
                        stop=(k == DOWN_PASSES - 1),
                    )
                x_psum_of[s] = x_psum

        def add_residual(g, i):
            n = len(GROUPS[g])
            if i >= n:
                return
            s = GROUPS[g][i]
            c, j = divmod(s, CHUNK_TILES)
            if j == 0:
                x_sb = x_pool.tile([P, CHUNK_TILES, E], F32)
                x_of[c] = x_sb
            nc.vector.tensor_tensor(
                out=x_of[c][:, j, :],
                in0=x_psum_of[s][:],
                in1=res_of[c][:, j, :],
                op=ALU.add,
            )
            if c >= SHORT_STORES and i == n - 1:
                nc.sync.dma_start(out=group_view(x_rows, GROUPS[g]), in_=x_of[c][:, j - n + 1 : j + 1, :])
            elif c < SHORT_STORES and j == CHUNK_TILES - 1:
                nc.sync.dma_start(out=chunk_view(x_rows, c), in_=x_of[c][:])

        def sum_squares(g, i):
            if i >= len(GROUPS[g]):
                return
            if i == 0:
                sum_sq = stat_pool.tile([P, 2], F32)
                sum_of[g] = sum_sq
            squares = square_pool.tile([P, E], BF16)
            c, j = divmod(GROUPS[g][i], CHUNK_TILES)
            nc.scalar.activation(
                out=squares[:], in_=x_of[c][:, j, :], func=ACT.Square, accum_out=sum_of[g][:, i : i + 1]
            )

        def inverse_rms(g):
            n = len(GROUPS[g])
            rstd = stat_pool.tile([P, 2], F32)
            nc.scalar.activation(
                out=rstd[:, :n], in_=sum_of[g][:, :n], func=ACT.Abs_reciprocal_sqrt, scale=1.0 / E, bias=eps[:]
            )
            rstd_of[g] = rstd

        def normalise(g, i):
            if i >= len(GROUPS[g]):
                return
            if g not in h_of:
                h_sb = h_pool.tile([P, 2, E], BF16)
                h_of[g] = h_sb
            c, j = divmod(GROUPS[g][i], CHUNK_TILES)
            nc.vector.scalar_tensor_tensor(
                out=h_of[g][:, i, :].rearrange("p (u j) -> p u j", u=2),
                in0=x_of[c][:, j, :].rearrange("p (j u) -> p u j", u=2),
                scalar=rstd_of[g][:, i : i + 1],
                in1=gain[:].rearrange("p (j u) -> p u j", u=2),
                op0=ALU.mult,
                op1=ALU.mult,
            )

        def transpose_h(g):
            hT = psum_h.tile([P, 2, 2 * P], F32)
            for i in range(len(GROUPS[g])):
                h_words = h_of[g][:, i, :].bitcast(F32)
                for u in range(2):
                    cols = slice(u * P, (u + 1) * P)
                    nc.tensor.transpose(hT[:, i, cols], h_words[:, cols], ident[:])
            hT_of[g] = hT

        def group_h(g):
            n = len(GROUPS[g])
            h_grouped = grouped_pool.tile([P, 2, E], BF16, align_bytes=64)
            nc.scalar.copy(
                out=h_grouped[:, :n, :].bitcast(F32).rearrange("p i (r u) -> p i r u", u=2),
                in_=hT_of[g][:, :n, :].rearrange("p i (u r) -> p i r u", u=2),
            )
            h_grouped_of[g] = h_grouped

        def quantise_h(g):
            n = len(GROUPS[g])
            h_codes = mx_pool.tile([P, 2 * P], U32, align_bytes=64)
            h_scales = mx_pool.tile([P, 2 * P], U8, align_bytes=64)
            nc.vector.quantize_mx(
                out=h_codes[:, : n * P].bitcast(FP8X4),
                scales=h_scales[:, : n * P],
                in_=h_grouped_of[g][:].rearrange("p i k -> p (i k)")[:, : n * E],
            )
            h_mx_of[g] = (h_codes, h_scales)

        def project_kv(g):
            h_codes, h_scales = h_mx_of[g]
            kv_psum = psum_kv.tile([P, 2, 2 * KV], F32)
            for i in range(len(GROUPS[g])):
                cols = slice(i * P, (i + 1) * P)
                nc.tensor.matmul_mx(
                    out=kv_psum[:, i, :],
                    lhsT=h_codes[:, cols].bitcast(FP8X4),
                    lhsT_scale=h_scales[:, cols],
                    rhs=wkv_codes[:].bitcast(FP8X4),
                    rhs_scale=wkv_scales[:],
                    start=True,
                    stop=True,
                )
            kv_psum_of[g] = kv_psum

        def store_kv(g):
            n = len(GROUPS[g])
            c, j = divmod(GROUPS[g][0], CHUNK_TILES)
            if j == 0:
                kv_sb = kv_pool.tile([P, 2, CHUNK_TILES, KV], F32)
                kv_of[c] = kv_sb
            nc.scalar.copy(
                out=kv_of[c][:, :, j : j + n, :].rearrange("p o i d -> p i o d"),
                in_=kv_psum_of[g][:, :n, :].rearrange("p i (o d) -> p i o d", o=2),
            )
            for o, rows in enumerate((k_rows, v_rows)):
                if c >= SHORT_STORES:
                    nc.sync.dma_start(out=group_view(rows, GROUPS[g]), in_=kv_of[c][:, o, j : j + n, :])
                elif j + n == CHUNK_TILES:
                    nc.sync.dma_start(out=chunk_view(rows, c), in_=kv_of[c][:, o])

        def run(stage, g, *which):
            if 0 <= g < len(GROUPS):
                stage(g, *which)

        def a_upto(t):
            return min(TILES, 7 + GROUPS[min(t, len(GROUPS) - 1)][-1]) if t >= 0 else 4

        def step(t):
            tiles = range(a_upto(t - 1), a_upto(t))
            run(transpose_h, t - 2)
            for s in tiles:
                transpose_a(s)
            run(add_residual, t, 0)
            run(add_residual, t, 1)
            run(store_kv, t - 4)
            run(group_h, t - 2)
            run(sum_squares, t, 0)
            run(sum_squares, t, 1)
            for s in tiles:
                group_a(s)
            run(inverse_rms, t)
            run(quantise_a, t + 2)
            run(normalise, t - 1, 0)
            run(normalise, t - 1, 1)
            run(quantise_h, t - 2)
            run(project_down, t + 1)
            run(project_kv, t - 3)

        warm_up(8)
        group_wd(nc.vector.tensor_copy, 0, 0)
        group_wd(nc.vector.tensor_copy, 0, 1)
        quantise_wd(0)
        group_wd(nc.vector.tensor_copy, 1, 0)
        group_wd(nc.vector.tensor_copy, 1, 1)
        for s in range(a_upto(-1)):
            transpose_a(s)
            if s == 0:
                warm_up(2)
            group_a(s)
            if s == 0:
                quantise_a(0)
                quantise_wd(1)
            if s == 3:
                project_down(0)
            if s == 1:
                quantise_a(1)
        for t in range(0, len(GROUPS) + 5):
            step(t)
            if t == 0:
                prepare_norm_and_kv()
